import numpy as np
import ml_dtypes


def mxq(x, axis, fmt="e4m3"):
    dtype, down = {"e4m3": (ml_dtypes.float8_e4m3fn, 7), "e5m2": (ml_dtypes.float8_e5m2, 14)}[fmt]
    v = np.moveaxis(np.asarray(x, np.float32).astype(ml_dtypes.bfloat16).astype(np.float64), axis, -1)
    blocks = v.reshape(v.shape[:-1] + (-1, 32))
    amax = np.abs(blocks).max(-1, keepdims=True)
    byte = np.maximum(np.where(amax > 0, np.frexp(amax)[1] - 1 + 127, 0) - down, 1)
    scale = np.exp2(byte - 127.0)
    codes = (blocks / scale).astype(np.float32).astype(dtype).astype(np.float64)
    return np.moveaxis((codes * scale).reshape(v.shape), -1, axis)


WIDE = False


def mx_kscale(k):
    if not WIDE:
        return np.ones(k)
    levels = np.array([10, -10, 5, -5, 0])
    a = np.random.permutation(np.resize(levels, k // 512 * 4)).reshape(k // 512, 4)
    idx = np.arange(k)
    return np.exp2(a[idx // 512, idx % 128 // 32])


BF16 = ml_dtypes.bfloat16


def bf(x):
    return np.asarray(x, np.float32).astype(BF16)


def f64(x):
    return np.asarray(x).astype(np.float64)


E2M1 = np.array([0.0, 0.5, 1.0, 1.5, 2.0, 3.0, 4.0, 6.0, -0.0, -0.5, -1.0, -1.5, -2.0, -3.0, -4.0, -6.0])


def pack_weight(w, fmt):
    k, n = w.shape
    w = f64(bf(w)).reshape(k // 32, 32, n)
    amax = np.abs(w).max(1)
    if fmt == "e4m3":
        byte = np.frexp(amax)[1] - 1 + 127 - 7
    else:
        mant, ex = np.frexp(amax / 6.0)
        byte = np.where(mant > 0.5, ex, ex - 1) + 127
    byte = np.clip(np.where(amax > 0, byte, 1), 1, 254)
    scaled = (w * np.exp2(127.0 - byte)[:, None, :]).reshape(k, n).astype(np.float32)
    by_word = np.ascontiguousarray(scaled.reshape(k // 512, 128, 4, n).transpose(0, 1, 3, 2))
    if fmt == "e4m3":
        words = by_word.astype(ml_dtypes.float8_e4m3fn).view(np.uint8)
    else:
        c = by_word.astype(ml_dtypes.float4_e2m1fn).view(np.uint8) & 0xF
        words = c[..., 0::2] | (c[..., 1::2] << 4)
    return np.ascontiguousarray(words), np.ascontiguousarray(byte.astype(np.uint8).reshape(k // 512, 16, n))


def unpack_weight(words, scales, fmt):
    g, p, n, _ = words.shape
    if fmt == "e4m3":
        vals = np.ascontiguousarray(words).view(ml_dtypes.float8_e4m3fn).astype(np.float64)
    else:
        nib = np.empty((g, p, n, 4), np.uint8)
        nib[..., 0::2] = words & 0xF
        nib[..., 1::2] = words >> 4
        vals = E2M1[nib]
    vals = vals * np.repeat(np.exp2(scales.astype(np.float64) - 127.0), 8, axis=1)[..., None]
    return vals.transpose(0, 1, 3, 2).reshape(g * 512, n)

def pack4(w):
    words, scales = pack_weight(w, "e2m1")
    return words.reshape(words.shape[0], 128, -1), scales


def unpack4(words, scales):
    return unpack_weight(words.reshape(words.shape[0], 128, -1, 2), scales, "e2m1")


B, T, D, NH, NG = 2, 64, 1024, 8, 4
GH = (D // NH) * NG
JIT = 0.06


def angles(t, d):
    i = np.arange(d // 2, dtype=np.float64)
    theta = (10000.0 ** (-(2.0 * (i - 1.0)))) / d
    return np.arange(t, dtype=np.float64)[:, None] * theta[None, :]


def rope(y, cos, sin):
    ye, yo = y[..., 0::2], y[..., 1::2]
    oe = ye * cos + yo * sin
    oo = -ye * sin + yo * cos
    return np.stack([oe, oo], axis=-1).reshape(y.shape)


def setup_inputs():
    s = mx_kscale(D)
    aq = angles(T, D) + JIT * np.random.standard_normal((T, D // 2))
    ak = angles(T, GH) + JIT * np.random.standard_normal((T, GH // 2))
    x = bf(np.random.standard_normal((B, T, D)) * s)
    Wq_words, Wq_scales = pack4(np.random.standard_normal((D, D)) / np.sqrt(D) / s[:, None])
    Wk_words, Wk_scales = pack4(np.random.standard_normal((D, GH)) / np.sqrt(D) / s[:, None])
    Wv_words, Wv_scales = pack4(np.random.standard_normal((D, GH)) / np.sqrt(D) / s[:, None])
    return {"x": x,
            "Wq_words": Wq_words, "Wq_scales": Wq_scales,
            "Wk_words": Wk_words, "Wk_scales": Wk_scales,
            "Wv_words": Wv_words, "Wv_scales": Wv_scales,
            "cos_q": bf(np.cos(aq)), "sin_q": bf(np.sin(aq)),
            "cos_k": bf(np.cos(ak)), "sin_k": bf(np.sin(ak))}


def reference(x, Wq_words, Wq_scales, Wk_words, Wk_scales, Wv_words, Wv_scales, cos_q, sin_q, cos_k, sin_k):
    xq = mxq(f64(x), 2, "e4m3")
    q = rope(xq @ unpack4(Wq_words, Wq_scales), f64(cos_q), f64(sin_q))
    k = rope(xq @ unpack4(Wk_words, Wk_scales), f64(cos_k), f64(sin_k))
    v = xq @ unpack4(Wv_words, Wv_scales)
    return q, k, v

@@ -1,0 +1,154 @@
+import concourse.mybir as mybir
+from concourse.masks import make_identity
+
+F32 = mybir.dt.float32
+BF16 = mybir.dt.bfloat16
+I32 = mybir.dt.int32
+U32 = mybir.dt.uint32
+U8 = mybir.dt.uint8
+FP8X4 = mybir.dt.float8_e4m3fn_x4
+FP4X4 = mybir.dt.float4_e2m1fn_x4
+MULT = mybir.AluOpType.mult
+ADD = mybir.AluOpType.add
+
+P = 128
+PACK = 4
+K_PASS = P * PACK
+TOKENS = 128
+POSITIONS = 64
+D_MODEL = 1024
+PASSES = D_MODEL // K_PASS
+Q_WIDTH = 1024
+KV_WIDTH = 512
+FEATURES = Q_WIDTH + 2 * KV_WIDTH
+BANK = 512
+BANKS = FEATURES // BANK
+ROTATED_BANKS = (Q_WIDTH + KV_WIDTH) // BANK
+PAIRS = BANK // 2
+WORDS_PER_PASS = K_PASS // 2
+
+FLOPS = 2 * TOKENS * D_MODEL * FEATURES
+
+
+def tile_selfattn_pa_s_kernel(
+    tc,
+    x,
+    Wq_words,
+    Wq_scales,
+    Wk_words,
+    Wk_scales,
+    Wv_words,
+    Wv_scales,
+    cos_q,
+    sin_q,
+    cos_k,
+    sin_k,
+    out_0,
+    out_1,
+    out_2,
+):
+    nc = tc.nc
+    q_out = out_0.flatten_outer_dims()
+    bank_out = [q_out[:, 0:BANK], q_out[:, BANK : 2 * BANK], out_1.flatten_outer_dims(), out_2.flatten_outer_dims()]
+
+    with (
+        tc.tile_pool(name="keep", bufs=1) as keep,
+        tc.psum_pool(name="psum", bufs=1) as psum,
+        tc.manual_schedule(),
+    ):
+        x_sb = keep.tile([TOKENS, D_MODEL], BF16)
+        identity = keep.tile([P, P], F32)
+        w_words = keep.tile([P, PASSES, 2 * FEATURES], U8, align_bytes=64)
+        w_scales = keep.tile([P, PASSES, FEATURES], U8, align_bytes=64)
+        cos_sb = keep.tile([TOKENS, ROTATED_BANKS * PAIRS], BF16)
+        sin_sb = keep.tile([TOKENS, ROTATED_BANKS * PAIRS], BF16)
+        grouped = keep.tile([P, PASSES, TOKENS, PACK], BF16, align_bytes=64)
+        x_codes = keep.tile([P, PASSES, TOKENS], U32, align_bytes=64)
+        x_scales = keep.tile([P, PASSES, TOKENS], U8, align_bytes=64)
+
+        def load_table(table_sb, table, first_pair):
+            for b in range(TOKENS // POSITIONS):
+                nc.sync.dma_start(
+                    out=table_sb[POSITIONS * b : POSITIONS * (b + 1), first_pair : first_pair + table.shape[1]],
+                    in_=table,
+                )
+
+        def load_weight(words, scales, first, width):
+            for r in range(4):
+                nc.sync.dma_start(
+                    out=w_scales[r:P:32, :, first : first + width].bitcast(I32),
+                    in_=scales[:, r:16:4, :].bitcast(I32).rearrange("g c n -> c g n"),
+                )
+            nc.sync.dma_start(
+                out=w_words[:, :, 2 * first : 2 * (first + width)].bitcast(I32),
+                in_=words.bitcast(I32).rearrange("g p n -> p g n"),
+            )
+
+        nc.vector.memset(w_scales[:].rearrange("p g n -> p (g n)").bitcast(I32), 0)
+        make_identity(nc, identity[:])
+        nc.sync.dma_start(out=x_sb[:], in_=x.flatten_outer_dims())
+        load_table(cos_sb, cos_q, 0)
+        load_weight(Wq_words, Wq_scales, 0, Q_WIDTH)
+        load_table(sin_sb, sin_q, 0)
+        load_weight(Wk_words, Wk_scales, Q_WIDTH, KV_WIDTH)
+        load_table(cos_sb, cos_k, Q_WIDTH // 2)
+        load_table(sin_sb, sin_k, Q_WIDTH // 2)
+        load_weight(Wv_words, Wv_scales, Q_WIDTH + KV_WIDTH, KV_WIDTH)
+
+        x_words = x_sb[:].bitcast(F32)
+        for g in range(PASSES):
+            x_t = psum.tile([P, 2, TOKENS], F32, name="x_t%d" % g)
+            for u in range(2):
+                nc.tensor.transpose(
+                    x_t[:, u, :],
+                    x_words[:, WORDS_PER_PASS * g + u : WORDS_PER_PASS * (g + 1) : 2],
+                    identity[:],
+                )
+            copy_out = nc.vector.tensor_copy if g == 0 else nc.scalar.copy
+            copy_out(
+                out=grouped[:, g].rearrange("p r t -> p (r t)").bitcast(F32).rearrange("p (r u) -> p r u", u=2),
+                in_=x_t[:].rearrange("p u r -> p r u"),
+            )
+        nc.vector.quantize_mx(
+            out=x_codes[:].rearrange("p g r -> p (g r)").bitcast(FP8X4),
+            scales=x_scales[:].rearrange("p g r -> p (g r)"),
+            in_=grouped[:].rearrange("p g r t -> p (g r t)"),
+        )
+
+        sums = []
+        for j in range(BANKS):
+            acc = psum.tile([TOKENS, BANK], F32, name="acc%d" % j)
+            for g in range(PASSES):
+                nc.tensor.matmul_mx(
+                    out=acc[:],
+                    lhsT=x_codes[:, g, :].bitcast(FP8X4),
+                    lhsT_scale=x_scales[:, g, :],
+                    rhs=w_words[:, g, 2 * BANK * j : 2 * BANK * (j + 1)].bitcast(FP4X4),
+                    rhs_scale=w_scales[:, g, BANK * j : BANK * (j + 1)],
+                    start=(g == 0),
+                    stop=(g == PASSES - 1),
+                )
+            sums.append(acc)
+
+        for j in range(ROTATED_BANKS):
+            y = sums[j][:].rearrange("p (i h) -> p i h", h=2)
+            cos_j = cos_sb[:, PAIRS * j : PAIRS * (j + 1)]
+            sin_j = sin_sb[:, PAIRS * j : PAIRS * (j + 1)]
+            straight = keep.tile([TOKENS, PAIRS, 2], F32, name="straight%d" % j)
+            nc.vector.tensor_tensor(
+                out=straight[:], in0=y, in1=cos_j.unsqueeze(2).to_broadcast([TOKENS, PAIRS, 2]), op=MULT
+            )
+            crossed = keep.tile([TOKENS, 2, PAIRS], F32, name="crossed%d" % j)
+            nc.vector.tensor_tensor(out=crossed[:, 0, :], in0=y[:, :, 1], in1=sin_j, op=MULT)
+            nc.vector.scalar_tensor_tensor(
+                out=crossed[:, 1, :], in0=y[:, :, 0], scalar=-1.0, in1=sin_j, op0=MULT, op1=MULT
+            )
+            rotated = keep.tile([TOKENS, PAIRS, 2], F32, name="rotated%d" % j)
+            nc.vector.tensor_tensor(
+                out=rotated[:], in0=straight[:], in1=crossed[:].rearrange("p h i -> p i h"), op=ADD
+            )
+            nc.sync.dma_start(out=bank_out[j], in_=rotated[:].rearrange("p i h -> p (i h)"))
+
+        v_sb = keep.tile([TOKENS, BANK], F32)
+        nc.scalar.copy(out=v_sb[:], in_=sums[BANKS - 1][:])
+        nc.scalar.dma_start(out=bank_out[BANKS - 1], in_=v_sb[:])

@@ -14,8 +14,9 @@ ADD = mybir.AluOpType.add
 P = 128
 PACK = 4
 K_PASS = P * PACK
-TOKENS = 128
+BATCHES = 2
 POSITIONS = 64
+TOKENS = BATCHES * POSITIONS
 D_MODEL = 1024
 PASSES = D_MODEL // K_PASS
 Q_WIDTH = 1024
@@ -48,8 +49,12 @@ def tile_selfattn_pa_s_kernel(
     out_2,
 ):
     nc = tc.nc
-    q_out = out_0.flatten_outer_dims()
-    bank_out = [q_out[:, 0:BANK], q_out[:, BANK : 2 * BANK], out_1.flatten_outer_dims(), out_2.flatten_outer_dims()]
+
+    def by_position(tokens_first):
+        return tokens_first.rearrange("b t d -> t b d")
+
+    q_out = by_position(out_0)
+    bank_out = [q_out[:, :, 0:BANK], q_out[:, :, BANK : 2 * BANK], by_position(out_1), by_position(out_2)]
 
     with (
         tc.tile_pool(name="keep", bufs=1) as keep,
@@ -66,12 +71,12 @@ def tile_selfattn_pa_s_kernel(
         x_codes = keep.tile([P, PASSES, TOKENS], U32, align_bytes=64)
         x_scales = keep.tile([P, PASSES, TOKENS], U8, align_bytes=64)
 
-        def load_table(table_sb, table, first_pair):
-            for b in range(TOKENS // POSITIONS):
-                nc.sync.dma_start(
-                    out=table_sb[POSITIONS * b : POSITIONS * (b + 1), first_pair : first_pair + table.shape[1]],
-                    in_=table,
-                )
+        def load_table(queue, table_sb, table, first_pair):
+            pairs = table.shape[1]
+            queue.dma_start(
+                out=table_sb[:, first_pair : first_pair + pairs],
+                in_=table.unsqueeze(1).to_broadcast([POSITIONS, BATCHES, pairs]),
+            )
 
         def load_weight(words, scales, first, width):
             for r in range(4):
@@ -86,13 +91,13 @@ def tile_selfattn_pa_s_kernel(
 
         nc.vector.memset(w_scales[:].rearrange("p g n -> p (g n)").bitcast(I32), 0)
         make_identity(nc, identity[:])
-        nc.sync.dma_start(out=x_sb[:], in_=x.flatten_outer_dims())
-        load_table(cos_sb, cos_q, 0)
+        nc.sync.dma_start(out=x_sb[:], in_=by_position(x))
         load_weight(Wq_words, Wq_scales, 0, Q_WIDTH)
-        load_table(sin_sb, sin_q, 0)
+        load_table(nc.sync, cos_sb, cos_q, 0)
+        load_table(nc.sync, sin_sb, sin_q, 0)
+        load_table(nc.gpsimd, cos_sb, cos_k, Q_WIDTH // 2)
+        load_table(nc.gpsimd, sin_sb, sin_k, Q_WIDTH // 2)
         load_weight(Wk_words, Wk_scales, Q_WIDTH, KV_WIDTH)
-        load_table(cos_sb, cos_k, Q_WIDTH // 2)
-        load_table(sin_sb, sin_k, Q_WIDTH // 2)
         load_weight(Wv_words, Wv_scales, Q_WIDTH + KV_WIDTH, KV_WIDTH)
 
         x_words = x_sb[:].bitcast(F32)
@@ -109,11 +114,11 @@ def tile_selfattn_pa_s_kernel(
                 out=grouped[:, g].rearrange("p r t -> p (r t)").bitcast(F32).rearrange("p (r u) -> p r u", u=2),
                 in_=x_t[:].rearrange("p u r -> p r u"),
             )
-        nc.vector.quantize_mx(
-            out=x_codes[:].rearrange("p g r -> p (g r)").bitcast(FP8X4),
-            scales=x_scales[:].rearrange("p g r -> p (g r)"),
-            in_=grouped[:].rearrange("p g r t -> p (g r t)"),
-        )
+            nc.vector.quantize_mx(
+                out=x_codes[:, g, :].bitcast(FP8X4),
+                scales=x_scales[:, g, :],
+                in_=grouped[:, g].rearrange("p r t -> p (r t)"),
+            )
 
         sums = []
         for j in range(BANKS):

@@ -63,42 +63,41 @@ def tile_selfattn_pa_s_kernel(
     ):
         x_sb = keep.tile([TOKENS, D_MODEL], BF16)
         identity = keep.tile([P, P], F32)
-        w_words = keep.tile([P, PASSES, 2 * FEATURES], U8, align_bytes=64)
-        w_scales = keep.tile([P, PASSES, FEATURES], U8, align_bytes=64)
         cos_sb = keep.tile([TOKENS, ROTATED_BANKS * PAIRS], BF16)
         sin_sb = keep.tile([TOKENS, ROTATED_BANKS * PAIRS], BF16)
         grouped = keep.tile([P, PASSES, TOKENS, PACK], BF16, align_bytes=64)
         x_codes = keep.tile([P, PASSES, TOKENS], U32, align_bytes=64)
         x_scales = keep.tile([P, PASSES, TOKENS], U8, align_bytes=64)
 
-        def load_table(queue, table_sb, table, first_pair):
+        def load_table(table_sb, table, first_pair):
             pairs = table.shape[1]
-            queue.dma_start(
+            nc.sync.dma_start(
                 out=table_sb[:, first_pair : first_pair + pairs],
                 in_=table.unsqueeze(1).to_broadcast([POSITIONS, BATCHES, pairs]),
             )
 
-        def load_weight(words, scales, first, width):
+        def load_weight(name, words, scales, width):
+            words_sb = keep.tile([P, PASSES, 2 * width], U8, name=name + "_words", align_bytes=64)
+            scales_sb = keep.tile([P, PASSES, width], U8, name=name + "_scales", align_bytes=64)
+            nc.vector.memset(scales_sb[:].rearrange("p g n -> p (g n)").bitcast(I32), 0)
             for r in range(4):
                 nc.sync.dma_start(
-                    out=w_scales[r:P:32, :, first : first + width].bitcast(I32),
+                    out=scales_sb[r:P:32, :, :].bitcast(I32),
                     in_=scales[:, r:16:4, :].bitcast(I32).rearrange("g c n -> c g n"),
                 )
-            nc.sync.dma_start(
-                out=w_words[:, :, 2 * first : 2 * (first + width)].bitcast(I32),
-                in_=words.bitcast(I32).rearrange("g p n -> p g n"),
-            )
+            nc.sync.dma_start(out=words_sb[:].bitcast(I32), in_=words.bitcast(I32).rearrange("g p n -> p g n"))
+            return words_sb, scales_sb
 
-        nc.vector.memset(w_scales[:].rearrange("p g n -> p (g n)").bitcast(I32), 0)
         make_identity(nc, identity[:])
         nc.sync.dma_start(out=x_sb[:], in_=by_position(x))
-        load_weight(Wq_words, Wq_scales, 0, Q_WIDTH)
-        load_table(nc.sync, cos_sb, cos_q, 0)
-        load_table(nc.sync, sin_sb, sin_q, 0)
-        load_table(nc.gpsimd, cos_sb, cos_k, Q_WIDTH // 2)
-        load_table(nc.gpsimd, sin_sb, sin_k, Q_WIDTH // 2)
-        load_weight(Wk_words, Wk_scales, Q_WIDTH, KV_WIDTH)
-        load_weight(Wv_words, Wv_scales, Q_WIDTH + KV_WIDTH, KV_WIDTH)
+        wq = load_weight("wq", Wq_words, Wq_scales, Q_WIDTH)
+        load_table(cos_sb, cos_q, 0)
+        load_table(sin_sb, sin_q, 0)
+        wk = load_weight("wk", Wk_words, Wk_scales, KV_WIDTH)
+        load_table(cos_sb, cos_k, Q_WIDTH // 2)
+        load_table(sin_sb, sin_k, Q_WIDTH // 2)
+        wv = load_weight("wv", Wv_words, Wv_scales, KV_WIDTH)
+        bank_weight = [(wq, 0), (wq, BANK), (wk, 0), (wv, 0)]
 
         x_words = x_sb[:].bitcast(F32)
         for g in range(PASSES):
@@ -123,13 +122,14 @@ def tile_selfattn_pa_s_kernel(
         sums = []
         for j in range(BANKS):
             acc = psum.tile([TOKENS, BANK], F32, name="acc%d" % j)
+            (words_sb, scales_sb), first = bank_weight[j]
             for g in range(PASSES):
                 nc.tensor.matmul_mx(
                     out=acc[:],
                     lhsT=x_codes[:, g, :].bitcast(FP8X4),
                     lhsT_scale=x_scales[:, g, :],
-                    rhs=w_words[:, g, 2 * BANK * j : 2 * BANK * (j + 1)].bitcast(FP4X4),
-                    rhs_scale=w_scales[:, g, BANK * j : BANK * (j + 1)],
+                    rhs=words_sb[:, g, 2 * first : 2 * (first + BANK)].bitcast(FP4X4),
+                    rhs_scale=scales_sb[:, g, first : first + BANK],
                     start=(g == 0),
                     stop=(g == PASSES - 1),
                 )

@@ -148,8 +148,9 @@ def tile_selfattn_pa_s_kernel(
             nc.vector.scalar_tensor_tensor(
                 out=crossed[:, 1, :], in0=y[:, :, 0], scalar=-1.0, in1=sin_j, op0=MULT, op1=MULT
             )
+            adder = nc.gpsimd if j < ROTATED_BANKS - 1 else nc.vector
             rotated = keep.tile([TOKENS, PAIRS, 2], F32, name="rotated%d" % j)
-            nc.vector.tensor_tensor(
+            adder.tensor_tensor(
                 out=rotated[:], in0=straight[:], in1=crossed[:].rearrange("p h i -> p i h"), op=ADD
             )
             nc.sync.dma_start(out=bank_out[j], in_=rotated[:].rearrange("p i h -> p (i h)"))

@@ -27,6 +27,7 @@ BANKS = FEATURES // BANK
 ROTATED_BANKS = (Q_WIDTH + KV_WIDTH) // BANK
 PAIRS = BANK // 2
 WORDS_PER_PASS = K_PASS // 2
+WARM_MATMULS = 3
 
 FLOPS = 2 * TOKENS * D_MODEL * FEATURES
 
@@ -76,8 +77,7 @@ def tile_selfattn_pa_s_kernel(
                 in_=table.unsqueeze(1).to_broadcast([POSITIONS, BATCHES, pairs]),
             )
 
-        def load_weight(name, words, scales, width):
-            words_sb = keep.tile([P, PASSES, 2 * width], U8, name=name + "_words", align_bytes=64)
+        def load_scales(name, scales, width):
             scales_sb = keep.tile([P, PASSES, width], U8, name=name + "_scales", align_bytes=64)
             nc.vector.memset(scales_sb[:].rearrange("p g n -> p (g n)").bitcast(I32), 0)
             for r in range(4):
@@ -85,19 +85,38 @@ def tile_selfattn_pa_s_kernel(
                     out=scales_sb[r:P:32, :, :].bitcast(I32),
                     in_=scales[:, r:16:4, :].bitcast(I32).rearrange("g c n -> c g n"),
                 )
-            nc.sync.dma_start(out=words_sb[:].bitcast(I32), in_=words.bitcast(I32).rearrange("g p n -> p g n"))
-            return words_sb, scales_sb
+            return scales_sb
+
+        def load_words(name, words, first):
+            words_sb = keep.tile([P, PASSES, 2 * BANK], U8, name=name + "_words", align_bytes=64)
+            nc.sync.dma_start(
+                out=words_sb[:].bitcast(I32),
+                in_=words[:, :, 2 * first : 2 * (first + BANK)].bitcast(I32).rearrange("g p n -> p g n"),
+            )
+            return words_sb
 
         make_identity(nc, identity[:])
+        unread = psum.tile([P, P], F32)
+        for w in range(WARM_MATMULS):
+            nc.tensor.matmul(out=unread[:], lhsT=identity[:], rhs=identity[:], start=True, stop=True)
         nc.sync.dma_start(out=x_sb[:], in_=by_position(x))
-        wq = load_weight("wq", Wq_words, Wq_scales, Q_WIDTH)
+        wq_scales = load_scales("wq", Wq_scales, Q_WIDTH)
+        wq0_words = load_words("wq0", Wq_words, 0)
         load_table(cos_sb, cos_q, 0)
         load_table(sin_sb, sin_q, 0)
-        wk = load_weight("wk", Wk_words, Wk_scales, KV_WIDTH)
+        wq1_words = load_words("wq1", Wq_words, BANK)
+        wk_scales = load_scales("wk", Wk_scales, KV_WIDTH)
+        wk_words = load_words("wk", Wk_words, 0)
         load_table(cos_sb, cos_k, Q_WIDTH // 2)
         load_table(sin_sb, sin_k, Q_WIDTH // 2)
-        wv = load_weight("wv", Wv_words, Wv_scales, KV_WIDTH)
-        bank_weight = [(wq, 0), (wq, BANK), (wk, 0), (wv, 0)]
+        wv_scales = load_scales("wv", Wv_scales, KV_WIDTH)
+        wv_words = load_words("wv", Wv_words, 0)
+        bank_weight = [
+            (wq0_words, wq_scales, 0),
+            (wq1_words, wq_scales, BANK),
+            (wk_words, wk_scales, 0),
+            (wv_words, wv_scales, 0),
+        ]
 
         x_words = x_sb[:].bitcast(F32)
         for g in range(PASSES):
@@ -122,20 +141,20 @@ def tile_selfattn_pa_s_kernel(
         sums = []
         for j in range(BANKS):
             acc = psum.tile([TOKENS, BANK], F32, name="acc%d" % j)
-            (words_sb, scales_sb), first = bank_weight[j]
+            words_sb, scales_sb, first = bank_weight[j]
             for g in range(PASSES):
                 nc.tensor.matmul_mx(
                     out=acc[:],
                     lhsT=x_codes[:, g, :].bitcast(FP8X4),
                     lhsT_scale=x_scales[:, g, :],
-                    rhs=words_sb[:, g, 2 * first : 2 * (first + BANK)].bitcast(FP4X4),
+                    rhs=words_sb[:, g, :].bitcast(FP4X4),
                     rhs_scale=scales_sb[:, g, first : first + BANK],
                     start=(g == 0),
                     stop=(g == PASSES - 1),
                 )
             sums.append(acc)
 
-        for j in range(ROTATED_BANKS):
+        def rotate(j):
             y = sums[j][:].rearrange("p (i h) -> p i h", h=2)
             cos_j = cos_sb[:, PAIRS * j : PAIRS * (j + 1)]
             sin_j = sin_sb[:, PAIRS * j : PAIRS * (j + 1)]
@@ -157,4 +176,7 @@ def tile_selfattn_pa_s_kernel(
 
         v_sb = keep.tile([TOKENS, BANK], F32)
         nc.scalar.copy(out=v_sb[:], in_=sums[BANKS - 1][:])
-        nc.scalar.dma_start(out=bank_out[BANKS - 1], in_=v_sb[:])
+        for j in range(ROTATED_BANKS - 1):
+            rotate(j)
+        nc.sync.dma_start(out=bank_out[BANKS - 1], in_=v_sb[:])
+        rotate(ROTATED_BANKS - 1)

@@ -27,7 +27,7 @@ BANKS = FEATURES // BANK
 ROTATED_BANKS = (Q_WIDTH + KV_WIDTH) // BANK
 PAIRS = BANK // 2
 WORDS_PER_PASS = K_PASS // 2
-WARM_MATMULS = 3
+WARM_MATMULS = 2
 
 FLOPS = 2 * TOKENS * D_MODEL * FEATURES
 
@@ -62,17 +62,18 @@ def tile_selfattn_pa_s_kernel(
         tc.psum_pool(name="psum", bufs=1) as psum,
         tc.manual_schedule(),
     ):
-        x_sb = keep.tile([TOKENS, D_MODEL], BF16)
+        x_sb = [keep.tile([TOKENS, K_PASS], BF16, name="x_sb%d" % g) for g in range(PASSES)]
         identity = keep.tile([P, P], F32)
         cos_sb = keep.tile([TOKENS, ROTATED_BANKS * PAIRS], BF16)
         sin_sb = keep.tile([TOKENS, ROTATED_BANKS * PAIRS], BF16)
+        signed_sin = keep.tile([TOKENS, ROTATED_BANKS * PAIRS, 2], BF16)
         grouped = keep.tile([P, PASSES, TOKENS, PACK], BF16, align_bytes=64)
         x_codes = keep.tile([P, PASSES, TOKENS], U32, align_bytes=64)
         x_scales = keep.tile([P, PASSES, TOKENS], U8, align_bytes=64)
 
-        def load_table(table_sb, table, first_pair):
+        def load_table(queue, table_sb, table, first_pair):
             pairs = table.shape[1]
-            nc.sync.dma_start(
+            queue.dma_start(
                 out=table_sb[:, first_pair : first_pair + pairs],
                 in_=table.unsqueeze(1).to_broadcast([POSITIONS, BATCHES, pairs]),
             )
@@ -99,18 +100,19 @@ def tile_selfattn_pa_s_kernel(
         unread = psum.tile([P, P], F32)
         for w in range(WARM_MATMULS):
             nc.tensor.matmul(out=unread[:], lhsT=identity[:], rhs=identity[:], start=True, stop=True)
-        nc.sync.dma_start(out=x_sb[:], in_=by_position(x))
-        wq_scales = load_scales("wq", Wq_scales, Q_WIDTH)
+        for g in range(PASSES):
+            nc.sync.dma_start(out=x_sb[g][:], in_=by_position(x)[:, :, K_PASS * g : K_PASS * (g + 1)])
         wq0_words = load_words("wq0", Wq_words, 0)
-        load_table(cos_sb, cos_q, 0)
-        load_table(sin_sb, sin_q, 0)
+        wq_scales = load_scales("wq", Wq_scales, Q_WIDTH)
+        load_table(nc.sync, sin_sb, sin_q, 0)
+        load_table(nc.sync, cos_sb, cos_q, 0)
+        load_table(nc.gpsimd, sin_sb, sin_k, Q_WIDTH // 2)
+        load_table(nc.gpsimd, cos_sb, cos_k, Q_WIDTH // 2)
         wq1_words = load_words("wq1", Wq_words, BANK)
         wk_scales = load_scales("wk", Wk_scales, KV_WIDTH)
         wk_words = load_words("wk", Wk_words, 0)
-        load_table(cos_sb, cos_k, Q_WIDTH // 2)
-        load_table(sin_sb, sin_k, Q_WIDTH // 2)
-        wv_scales = load_scales("wv", Wv_scales, KV_WIDTH)
         wv_words = load_words("wv", Wv_words, 0)
+        wv_scales = load_scales("wv", Wv_scales, KV_WIDTH)
         bank_weight = [
             (wq0_words, wq_scales, 0),
             (wq1_words, wq_scales, BANK),
@@ -118,13 +120,13 @@ def tile_selfattn_pa_s_kernel(
             (wv_words, wv_scales, 0),
         ]
 
-        x_words = x_sb[:].bitcast(F32)
         for g in range(PASSES):
+            x_words = x_sb[g][:].bitcast(F32)
             x_t = psum.tile([P, 2, TOKENS], F32, name="x_t%d" % g)
             for u in range(2):
                 nc.tensor.transpose(
                     x_t[:, u, :],
-                    x_words[:, WORDS_PER_PASS * g + u : WORDS_PER_PASS * (g + 1) : 2],
+                    x_words[:, u:WORDS_PER_PASS:2],
                     identity[:],
                 )
             copy_out = nc.vector.tensor_copy if g == 0 else nc.scalar.copy
@@ -154,26 +156,27 @@ def tile_selfattn_pa_s_kernel(
                 )
             sums.append(acc)
 
+        def sign_sin(j):
+            pairs_j = slice(PAIRS * j, PAIRS * (j + 1))
+            nc.scalar.copy(out=signed_sin[:, pairs_j, 0], in_=sin_sb[:, pairs_j])
+            nc.scalar.mul(out=signed_sin[:, pairs_j, 1], in_=sin_sb[:, pairs_j], mul=-1.0)
+
         def rotate(j):
             y = sums[j][:].rearrange("p (i h) -> p i h", h=2)
-            cos_j = cos_sb[:, PAIRS * j : PAIRS * (j + 1)]
-            sin_j = sin_sb[:, PAIRS * j : PAIRS * (j + 1)]
+            pairs_j = slice(PAIRS * j, PAIRS * (j + 1))
             straight = keep.tile([TOKENS, PAIRS, 2], F32, name="straight%d" % j)
             nc.vector.tensor_tensor(
-                out=straight[:], in0=y, in1=cos_j.unsqueeze(2).to_broadcast([TOKENS, PAIRS, 2]), op=MULT
+                out=straight[:], in0=y, in1=cos_sb[:, pairs_j].unsqueeze(2).to_broadcast([TOKENS, PAIRS, 2]), op=MULT
             )
-            crossed = keep.tile([TOKENS, 2, PAIRS], F32, name="crossed%d" % j)
-            nc.vector.tensor_tensor(out=crossed[:, 0, :], in0=y[:, :, 1], in1=sin_j, op=MULT)
-            nc.vector.scalar_tensor_tensor(
-                out=crossed[:, 1, :], in0=y[:, :, 0], scalar=-1.0, in1=sin_j, op0=MULT, op1=MULT
-            )
+            crossed = keep.tile([TOKENS, PAIRS, 2], F32, name="crossed%d" % j)
+            nc.vector.tensor_tensor(out=crossed[:], in0=y[:, :, ::-1], in1=signed_sin[:, pairs_j, :], op=MULT)
             adder = nc.gpsimd if j < ROTATED_BANKS - 1 else nc.vector
             rotated = keep.tile([TOKENS, PAIRS, 2], F32, name="rotated%d" % j)
-            adder.tensor_tensor(
-                out=rotated[:], in0=straight[:], in1=crossed[:].rearrange("p h i -> p i h"), op=ADD
-            )
+            adder.tensor_tensor(out=rotated[:], in0=straight[:], in1=crossed[:], op=ADD)
             nc.sync.dma_start(out=bank_out[j], in_=rotated[:].rearrange("p i h -> p (i h)"))
 
+        for j in range(ROTATED_BANKS):
+            sign_sin(j)
         v_sb = keep.tile([TOKENS, BANK], F32)
         nc.scalar.copy(out=v_sb[:], in_=sums[BANKS - 1][:])
         for j in range(ROTATED_BANKS - 1):

@@ -27,7 +27,8 @@ BANKS = FEATURES // BANK
 ROTATED_BANKS = (Q_WIDTH + KV_WIDTH) // BANK
 PAIRS = BANK // 2
 WORDS_PER_PASS = K_PASS // 2
-WARM_MATMULS = 2
+WARM_BEFORE_X = 3
+WARM_AFTER_TRANSPOSES = 1
 
 FLOPS = 2 * TOKENS * D_MODEL * FEATURES
 
@@ -97,9 +98,15 @@ def tile_selfattn_pa_s_kernel(
             return words_sb
 
         make_identity(nc, identity[:])
+        zeros = keep.tile([P, P], F32)
+        nc.vector.memset(zeros[:], 0.0)
         unread = psum.tile([P, P], F32)
-        for w in range(WARM_MATMULS):
-            nc.tensor.matmul(out=unread[:], lhsT=identity[:], rhs=identity[:], start=True, stop=True)
+
+        def keep_tensor_busy(matmuls):
+            for w in range(matmuls):
+                nc.tensor.matmul(out=unread[:], lhsT=zeros[:], rhs=zeros[:], start=True, stop=True)
+
+        keep_tensor_busy(WARM_BEFORE_X)
         for g in range(PASSES):
             nc.sync.dma_start(out=x_sb[g][:], in_=by_position(x)[:, :, K_PASS * g : K_PASS * (g + 1)])
         wq0_words = load_words("wq0", Wq_words, 0)
@@ -139,6 +146,8 @@ def tile_selfattn_pa_s_kernel(
                 scales=x_scales[:, g, :],
                 in_=grouped[:, g].rearrange("p r t -> p (r t)"),
             )
+
+        keep_tensor_busy(WARM_AFTER_TRANSPOSES)
 
         sums = []
         for j in range(BANKS):

@@ -136,8 +136,7 @@ def tile_selfattn_pa_s_kernel(
                     x_words[:, u:WORDS_PER_PASS:2],
                     identity[:],
                 )
-            copy_out = nc.vector.tensor_copy if g == 0 else nc.scalar.copy
-            copy_out(
+            nc.scalar.copy(
                 out=grouped[:, g].rearrange("p r t -> p (r t)").bitcast(F32).rearrange("p (r u) -> p r u", u=2),
                 in_=x_t[:].rearrange("p u r -> p r u"),
             )

@@ -169,25 +169,33 @@ def tile_selfattn_pa_s_kernel(
             nc.scalar.copy(out=signed_sin[:, pairs_j, 0], in_=sin_sb[:, pairs_j])
             nc.scalar.mul(out=signed_sin[:, pairs_j, 1], in_=sin_sb[:, pairs_j], mul=-1.0)
 
-        def rotate(j):
+        def rotate(j, pieces):
             y = sums[j][:].rearrange("p (i h) -> p i h", h=2)
-            pairs_j = slice(PAIRS * j, PAIRS * (j + 1))
             straight = keep.tile([TOKENS, PAIRS, 2], F32, name="straight%d" % j)
-            nc.vector.tensor_tensor(
-                out=straight[:], in0=y, in1=cos_sb[:, pairs_j].unsqueeze(2).to_broadcast([TOKENS, PAIRS, 2]), op=MULT
-            )
             crossed = keep.tile([TOKENS, PAIRS, 2], F32, name="crossed%d" % j)
-            nc.vector.tensor_tensor(out=crossed[:], in0=y[:, :, ::-1], in1=signed_sin[:, pairs_j, :], op=MULT)
-            adder = nc.gpsimd if j < ROTATED_BANKS - 1 else nc.vector
             rotated = keep.tile([TOKENS, PAIRS, 2], F32, name="rotated%d" % j)
-            adder.tensor_tensor(out=rotated[:], in0=straight[:], in1=crossed[:], op=ADD)
+            adder = nc.gpsimd if j < ROTATED_BANKS - 1 else nc.vector
+            width = PAIRS // pieces
+            for c in range(pieces):
+                part = slice(width * c, width * (c + 1))
+                table_part = slice(PAIRS * j + width * c, PAIRS * j + width * (c + 1))
+                nc.vector.tensor_tensor(
+                    out=straight[:, part, :],
+                    in0=y[:, part, :],
+                    in1=cos_sb[:, table_part].unsqueeze(2).to_broadcast([TOKENS, width, 2]),
+                    op=MULT,
+                )
+                nc.vector.tensor_tensor(
+                    out=crossed[:, part, :], in0=y[:, part, ::-1], in1=signed_sin[:, table_part, :], op=MULT
+                )
+                adder.tensor_tensor(out=rotated[:, part, :], in0=straight[:, part, :], in1=crossed[:, part, :], op=ADD)
             nc.sync.dma_start(out=bank_out[j], in_=rotated[:].rearrange("p i h -> p (i h)"))
 
         for j in range(ROTATED_BANKS):
             sign_sin(j)
         v_sb = keep.tile([TOKENS, BANK], F32)
         nc.scalar.copy(out=v_sb[:], in_=sums[BANKS - 1][:])
-        for j in range(ROTATED_BANKS - 1):
-            rotate(j)
+        rotate(0, 2)
+        rotate(1, 2)
         nc.sync.dma_start(out=bank_out[BANKS - 1], in_=v_sb[:])
-        rotate(ROTATED_BANKS - 1)
+        rotate(2, 1)

@@ -27,6 +27,7 @@ BANKS = FEATURES // BANK
 ROTATED_BANKS = (Q_WIDTH + KV_WIDTH) // BANK
 PAIRS = BANK // 2
 WORDS_PER_PASS = K_PASS // 2
+NARROW = 128
 WARM_BEFORE_X = 3
 WARM_AFTER_TRANSPOSES = 1
 
@@ -66,8 +67,8 @@ def tile_selfattn_pa_s_kernel(
         x_sb = [keep.tile([TOKENS, K_PASS], BF16, name="x_sb%d" % g) for g in range(PASSES)]
         identity = keep.tile([P, P], F32)
         cos_sb = keep.tile([TOKENS, ROTATED_BANKS * PAIRS], BF16)
-        sin_sb = keep.tile([TOKENS, ROTATED_BANKS * PAIRS], BF16)
-        signed_sin = keep.tile([TOKENS, ROTATED_BANKS * PAIRS, 2], BF16)
+        signed_sin = keep.tile([TOKENS, 2, ROTATED_BANKS * PAIRS], BF16)
+        sin_sb = signed_sin[:, 0, :]
         grouped = keep.tile([P, PASSES, TOKENS, PACK], BF16, align_bytes=64)
         x_codes = keep.tile([P, PASSES, TOKENS], U32, align_bytes=64)
         x_scales = keep.tile([P, PASSES, TOKENS], U8, align_bytes=64)
@@ -147,55 +148,59 @@ def tile_selfattn_pa_s_kernel(
             )
 
         keep_tensor_busy(WARM_AFTER_TRANSPOSES)
+        nc.vector.tensor_scalar(
+            out=signed_sin[:, 1, 0 : Q_WIDTH // 2], in0=sin_sb[:, 0 : Q_WIDTH // 2], scalar1=-1.0, scalar2=None, op0=MULT
+        )
 
-        sums = []
-        for j in range(BANKS):
+        def multiply(acc, at, j, first, width, g):
+            words_sb, scales_sb, plane_first = bank_weight[j]
+            nc.tensor.matmul_mx(
+                out=acc[:, at : at + width],
+                lhsT=x_codes[:, g, :].bitcast(FP8X4),
+                lhsT_scale=x_scales[:, g, :],
+                rhs=words_sb[:, g, 2 * first : 2 * (first + width)].bitcast(FP4X4),
+                rhs_scale=scales_sb[:, g, plane_first + first : plane_first + first + width],
+                start=(g == 0),
+                stop=(g == PASSES - 1),
+            )
+
+        head = psum.tile([TOKENS, BANK], F32, name="head")
+        whole = psum.tile([TOKENS, BANK], F32, name="whole")
+        for g in range(PASSES):
+            multiply(head, 0, 0, 0, NARROW, g)
+            multiply(whole, 0, 0, 0, BANK, g)
+        sums = [None]
+        for j in range(1, BANKS):
             acc = psum.tile([TOKENS, BANK], F32, name="acc%d" % j)
-            words_sb, scales_sb, first = bank_weight[j]
             for g in range(PASSES):
-                nc.tensor.matmul_mx(
-                    out=acc[:],
-                    lhsT=x_codes[:, g, :].bitcast(FP8X4),
-                    lhsT_scale=x_scales[:, g, :],
-                    rhs=words_sb[:, g, :].bitcast(FP4X4),
-                    rhs_scale=scales_sb[:, g, first : first + BANK],
-                    start=(g == 0),
-                    stop=(g == PASSES - 1),
-                )
+                multiply(acc, 0, j, 0, BANK, g)
             sums.append(acc)
 
-        def sign_sin(j):
-            pairs_j = slice(PAIRS * j, PAIRS * (j + 1))
-            nc.scalar.copy(out=signed_sin[:, pairs_j, 0], in_=sin_sb[:, pairs_j])
-            nc.scalar.mul(out=signed_sin[:, pairs_j, 1], in_=sin_sb[:, pairs_j], mul=-1.0)
-
         def rotate(j, pieces):
-            y = sums[j][:].rearrange("p (i h) -> p i h", h=2)
             straight = keep.tile([TOKENS, PAIRS, 2], F32, name="straight%d" % j)
             crossed = keep.tile([TOKENS, PAIRS, 2], F32, name="crossed%d" % j)
             rotated = keep.tile([TOKENS, PAIRS, 2], F32, name="rotated%d" % j)
             adder = nc.gpsimd if j < ROTATED_BANKS - 1 else nc.vector
-            width = PAIRS // pieces
-            for c in range(pieces):
-                part = slice(width * c, width * (c + 1))
-                table_part = slice(PAIRS * j + width * c, PAIRS * j + width * (c + 1))
+            for columns, first_pair, width in pieces:
+                y = columns.rearrange("p (i h) -> p i h", h=2)
+                part = slice(first_pair, first_pair + width)
+                table_part = slice(PAIRS * j + first_pair, PAIRS * j + first_pair + width)
                 nc.vector.tensor_tensor(
                     out=straight[:, part, :],
-                    in0=y[:, part, :],
+                    in0=y,
                     in1=cos_sb[:, table_part].unsqueeze(2).to_broadcast([TOKENS, width, 2]),
                     op=MULT,
                 )
                 nc.vector.tensor_tensor(
-                    out=crossed[:, part, :], in0=y[:, part, ::-1], in1=signed_sin[:, table_part, :], op=MULT
+                    out=crossed[:, part, :], in0=y[:, :, ::-1], in1=signed_sin[:, :, table_part].rearrange("p h i -> p i h"), op=MULT
                 )
                 adder.tensor_tensor(out=rotated[:, part, :], in0=straight[:, part, :], in1=crossed[:, part, :], op=ADD)
             nc.sync.dma_start(out=bank_out[j], in_=rotated[:].rearrange("p i h -> p (i h)"))
 
-        for j in range(ROTATED_BANKS):
-            sign_sin(j)
+        nc.scalar.mul(out=signed_sin[:, 1, Q_WIDTH // 2 :], in_=sin_sb[:, Q_WIDTH // 2 :], mul=-1.0)
         v_sb = keep.tile([TOKENS, BANK], F32)
         nc.scalar.copy(out=v_sb[:], in_=sums[BANKS - 1][:])
-        rotate(0, 2)
-        rotate(1, 2)
+        rotate(0, [(head[:, 0:NARROW], 0, NARROW // 2), (whole[:, NARROW:BANK], NARROW // 2, (BANK - NARROW) // 2)])
+        rotate(1, [(sums[1][:, 0 : BANK // 2], 0, PAIRS // 2), (sums[1][:, BANK // 2 : BANK], PAIRS // 2, PAIRS // 2)])
         nc.sync.dma_start(out=bank_out[BANKS - 1], in_=v_sb[:])
-        rotate(2, 1)
+        rotate(2, [(sums[2][:], 0, PAIRS)])

@@ -28,7 +28,7 @@ ROTATED_BANKS = (Q_WIDTH + KV_WIDTH) // BANK
 PAIRS = BANK // 2
 WORDS_PER_PASS = K_PASS // 2
 NARROW = 128
-WARM_BEFORE_X = 3
+WARM_BEFORE_X = 2
 WARM_AFTER_TRANSPOSES = 1
 
 FLOPS = 2 * TOKENS * D_MODEL * FEATURES
@@ -98,14 +98,17 @@ def tile_selfattn_pa_s_kernel(
             )
             return words_sb
 
+        zeros = keep.tile([P, BANK // 2], F32)
+        nc.gpsimd.memset(zeros[:], 0.0)
         make_identity(nc, identity[:])
-        zeros = keep.tile([P, P], F32)
-        nc.vector.memset(zeros[:], 0.0)
-        unread = psum.tile([P, P], F32)
+        unread = psum.tile([P, BANK], F32)
+        nc.tensor.matmul(
+            out=unread[:], lhsT=zeros[:].bitcast(BF16)[:, 0:P], rhs=zeros[:].bitcast(BF16), start=True, stop=True
+        )
 
         def keep_tensor_busy(matmuls):
             for w in range(matmuls):
-                nc.tensor.matmul(out=unread[:], lhsT=zeros[:], rhs=zeros[:], start=True, stop=True)
+                nc.tensor.matmul(out=unread[:, 0:P], lhsT=zeros[:, 0:P], rhs=zeros[:, 0:P], start=True, stop=True)
 
         keep_tensor_busy(WARM_BEFORE_X)
         for g in range(PASSES):

@@ -101,7 +101,8 @@ def tile_selfattn_pa_s_kernel(
         zeros = keep.tile([P, BANK // 2], F32)
         nc.gpsimd.memset(zeros[:], 0.0)
         make_identity(nc, identity[:])
-        unread = psum.tile([P, BANK], F32)
+        head = psum.tile([TOKENS, BANK], F32, name="head")
+        unread = head
         nc.tensor.matmul(
             out=unread[:], lhsT=zeros[:].bitcast(BF16)[:, 0:P], rhs=zeros[:].bitcast(BF16), start=True, stop=True
         )
@@ -167,17 +168,23 @@ def tile_selfattn_pa_s_kernel(
                 stop=(g == PASSES - 1),
             )
 
-        head = psum.tile([TOKENS, BANK], F32, name="head")
         whole = psum.tile([TOKENS, BANK], F32, name="whole")
         for g in range(PASSES):
             multiply(head, 0, 0, 0, NARROW, g)
             multiply(whole, 0, 0, 0, BANK, g)
         sums = [None]
-        for j in range(1, BANKS):
+        for j in range(1, ROTATED_BANKS):
             acc = psum.tile([TOKENS, BANK], F32, name="acc%d" % j)
             for g in range(PASSES):
                 multiply(acc, 0, j, 0, BANK, g)
             sums.append(acc)
+        v_sums = []
+        for half in range(2):
+            acc = psum.tile([TOKENS, BANK], F32, name="v_acc%d" % half)
+            for at in range(0, BANK // 2, NARROW):
+                for g in range(PASSES):
+                    multiply(acc, at, BANKS - 1, half * (BANK // 2) + at, NARROW, g)
+            v_sums.append(acc)
 
         def rotate(j, pieces):
             straight = keep.tile([TOKENS, PAIRS, 2], F32, name="straight%d" % j)
@@ -202,7 +209,8 @@ def tile_selfattn_pa_s_kernel(
 
         nc.scalar.mul(out=signed_sin[:, 1, Q_WIDTH // 2 :], in_=sin_sb[:, Q_WIDTH // 2 :], mul=-1.0)
         v_sb = keep.tile([TOKENS, BANK], F32)
-        nc.scalar.copy(out=v_sb[:], in_=sums[BANKS - 1][:])
+        for half in range(2):
+            nc.scalar.copy(out=v_sb[:, half * (BANK // 2) : (half + 1) * (BANK // 2)], in_=v_sums[half][:, 0 : BANK // 2])
         rotate(0, [(head[:, 0:NARROW], 0, NARROW // 2), (whole[:, NARROW:BANK], NARROW // 2, (BANK - NARROW) // 2)])
         rotate(1, [(sums[1][:, 0 : BANK // 2], 0, PAIRS // 2), (sums[1][:, BANK // 2 : BANK], PAIRS // 2, PAIRS // 2)])
         nc.sync.dma_start(out=bank_out[BANKS - 1], in_=v_sb[:])

import concourse.mybir as mybir
from concourse.masks import make_identity

F32 = mybir.dt.float32
BF16 = mybir.dt.bfloat16
I32 = mybir.dt.int32
U32 = mybir.dt.uint32
U8 = mybir.dt.uint8
FP8X4 = mybir.dt.float8_e4m3fn_x4
FP4X4 = mybir.dt.float4_e2m1fn_x4
MULT = mybir.AluOpType.mult
ADD = mybir.AluOpType.add

P = 128
PACK = 4
K_PASS = P * PACK
BATCHES = 2
POSITIONS = 64
TOKENS = BATCHES * POSITIONS
D_MODEL = 1024
PASSES = D_MODEL // K_PASS
Q_WIDTH = 1024
KV_WIDTH = 512
FEATURES = Q_WIDTH + 2 * KV_WIDTH
BANK = 512
BANKS = FEATURES // BANK
ROTATED_BANKS = (Q_WIDTH + KV_WIDTH) // BANK
PAIRS = BANK // 2
WORDS_PER_PASS = K_PASS // 2
NARROW = 128
WARM_BEFORE_X = 2
WARM_AFTER_TRANSPOSES = 1

FLOPS = 2 * TOKENS * D_MODEL * FEATURES


def tile_selfattn_pa_s_kernel(
    tc,
    x,
    Wq_words,
    Wq_scales,
    Wk_words,
    Wk_scales,
    Wv_words,
    Wv_scales,
    cos_q,
    sin_q,
    cos_k,
    sin_k,
    out_0,
    out_1,
    out_2,
):
    nc = tc.nc

    def by_position(tokens_first):
        return tokens_first.rearrange("b t d -> t b d")

    q_out = by_position(out_0)
    bank_out = [q_out[:, :, 0:BANK], q_out[:, :, BANK : 2 * BANK], by_position(out_1), by_position(out_2)]

    with (
        tc.tile_pool(name="keep", bufs=1) as keep,
        tc.psum_pool(name="psum", bufs=1) as psum,
        tc.manual_schedule(),
    ):
        x_sb = [keep.tile([TOKENS, K_PASS], BF16, name="x_sb%d" % g) for g in range(PASSES)]
        identity = keep.tile([P, P], F32)
        cos_sb = keep.tile([TOKENS, ROTATED_BANKS * PAIRS], BF16)
        signed_sin = keep.tile([TOKENS, 2, ROTATED_BANKS * PAIRS], BF16)
        sin_sb = signed_sin[:, 0, :]
        grouped = keep.tile([P, PASSES, TOKENS, PACK], BF16, align_bytes=64)
        x_codes = keep.tile([P, PASSES, TOKENS], U32, align_bytes=64)
        x_scales = keep.tile([P, PASSES, TOKENS], U8, align_bytes=64)

        def load_table(queue, table_sb, table, first_pair):
            pairs = table.shape[1]
            queue.dma_start(
                out=table_sb[:, first_pair : first_pair + pairs],
                in_=table.unsqueeze(1).to_broadcast([POSITIONS, BATCHES, pairs]),
            )

        def load_scales(name, scales, width):
            scales_sb = keep.tile([P, PASSES, width], U8, name=name + "_scales", align_bytes=64)
            nc.vector.memset(scales_sb[:].rearrange("p g n -> p (g n)").bitcast(I32), 0)
            for r in range(4):
                nc.sync.dma_start(
                    out=scales_sb[r:P:32, :, :].bitcast(I32),
                    in_=scales[:, r:16:4, :].bitcast(I32).rearrange("g c n -> c g n"),
                )
            return scales_sb

        def load_words(name, words, first):
            words_sb = keep.tile([P, PASSES, 2 * BANK], U8, name=name + "_words", align_bytes=64)
            nc.sync.dma_start(
                out=words_sb[:].bitcast(I32),
                in_=words[:, :, 2 * first : 2 * (first + BANK)].bitcast(I32).rearrange("g p n -> p g n"),
            )
            return words_sb

        zeros = keep.tile([P, BANK // 2], F32)
        nc.gpsimd.memset(zeros[:], 0.0)
        make_identity(nc, identity[:])
        head = psum.tile([TOKENS, BANK], F32, name="head")
        unread = head
        nc.tensor.matmul(
            out=unread[:], lhsT=zeros[:].bitcast(BF16)[:, 0:P], rhs=zeros[:].bitcast(BF16), start=True, stop=True
        )

        def keep_tensor_busy(matmuls):
            for w in range(matmuls):
                nc.tensor.matmul(out=unread[:, 0:P], lhsT=zeros[:, 0:P], rhs=zeros[:, 0:P], start=True, stop=True)

        keep_tensor_busy(WARM_BEFORE_X)
        for g in range(PASSES):
            nc.sync.dma_start(out=x_sb[g][:], in_=by_position(x)[:, :, K_PASS * g : K_PASS * (g + 1)])
        wq0_words = load_words("wq0", Wq_words, 0)
        wq_scales = load_scales("wq", Wq_scales, Q_WIDTH)
        load_table(nc.sync, sin_sb, sin_q, 0)
        load_table(nc.sync, cos_sb, cos_q, 0)
        load_table(nc.gpsimd, sin_sb, sin_k, Q_WIDTH // 2)
        load_table(nc.gpsimd, cos_sb, cos_k, Q_WIDTH // 2)
        wq1_words = load_words("wq1", Wq_words, BANK)
        wk_scales = load_scales("wk", Wk_scales, KV_WIDTH)
        wk_words = load_words("wk", Wk_words, 0)
        wv_words = load_words("wv", Wv_words, 0)
        wv_scales = load_scales("wv", Wv_scales, KV_WIDTH)
        bank_weight = [
            (wq0_words, wq_scales, 0),
            (wq1_words, wq_scales, BANK),
            (wk_words, wk_scales, 0),
            (wv_words, wv_scales, 0),
        ]

        for g in range(PASSES):
            x_words = x_sb[g][:].bitcast(F32)
            x_t = psum.tile([P, 2, TOKENS], F32, name="x_t%d" % g)
            for u in range(2):
                nc.tensor.transpose(
                    x_t[:, u, :],
                    x_words[:, u:WORDS_PER_PASS:2],
                    identity[:],
                )
            nc.scalar.copy(
                out=grouped[:, g].rearrange("p r t -> p (r t)").bitcast(F32).rearrange("p (r u) -> p r u", u=2),
                in_=x_t[:].rearrange("p u r -> p r u"),
            )
            nc.vector.quantize_mx(
                out=x_codes[:, g, :].bitcast(FP8X4),
                scales=x_scales[:, g, :],
                in_=grouped[:, g].rearrange("p r t -> p (r t)"),
            )

        keep_tensor_busy(WARM_AFTER_TRANSPOSES)
        nc.vector.tensor_scalar(
            out=signed_sin[:, 1, 0 : Q_WIDTH // 2], in0=sin_sb[:, 0 : Q_WIDTH // 2], scalar1=-1.0, scalar2=None, op0=MULT
        )

        def multiply(acc, at, j, first, width, g):
            words_sb, scales_sb, plane_first = bank_weight[j]
            nc.tensor.matmul_mx(
                out=acc[:, at : at + width],
                lhsT=x_codes[:, g, :].bitcast(FP8X4),
                lhsT_scale=x_scales[:, g, :],
                rhs=words_sb[:, g, 2 * first : 2 * (first + width)].bitcast(FP4X4),
                rhs_scale=scales_sb[:, g, plane_first + first : plane_first + first + width],
                start=(g == 0),
                stop=(g == PASSES - 1),
            )

        whole = psum.tile([TOKENS, BANK], F32, name="whole")
        for g in range(PASSES):
            multiply(head, 0, 0, 0, NARROW, g)
            multiply(whole, 0, 0, 0, BANK, g)
        sums = [None]
        for j in range(1, ROTATED_BANKS):
            acc = psum.tile([TOKENS, BANK], F32, name="acc%d" % j)
            for g in range(PASSES):
                multiply(acc, 0, j, 0, BANK, g)
            sums.append(acc)
        v_sums = []
        for half in range(2):
            acc = psum.tile([TOKENS, BANK], F32, name="v_acc%d" % half)
            for at in range(0, BANK // 2, NARROW):
                for g in range(PASSES):
                    multiply(acc, at, BANKS - 1, half * (BANK // 2) + at, NARROW, g)
            v_sums.append(acc)

        def rotate(j, pieces):
            straight = keep.tile([TOKENS, PAIRS, 2], F32, name="straight%d" % j)
            crossed = keep.tile([TOKENS, PAIRS, 2], F32, name="crossed%d" % j)
            rotated = keep.tile([TOKENS, PAIRS, 2], F32, name="rotated%d" % j)
            adder = nc.gpsimd if j < ROTATED_BANKS - 1 else nc.vector
            for columns, first_pair, width in pieces:
                y = columns.rearrange("p (i h) -> p i h", h=2)
                part = slice(first_pair, first_pair + width)
                table_part = slice(PAIRS * j + first_pair, PAIRS * j + first_pair + width)
                nc.vector.tensor_tensor(
                    out=straight[:, part, :],
                    in0=y,
                    in1=cos_sb[:, table_part].unsqueeze(2).to_broadcast([TOKENS, width, 2]),
                    op=MULT,
                )
                nc.vector.tensor_tensor(
                    out=crossed[:, part, :], in0=y[:, :, ::-1], in1=signed_sin[:, :, table_part].rearrange("p h i -> p i h"), op=MULT
                )
                adder.tensor_tensor(out=rotated[:, part, :], in0=straight[:, part, :], in1=crossed[:, part, :], op=ADD)
            nc.sync.dma_start(out=bank_out[j], in_=rotated[:].rearrange("p i h -> p (i h)"))

        nc.scalar.mul(out=signed_sin[:, 1, Q_WIDTH // 2 :], in_=sin_sb[:, Q_WIDTH // 2 :], mul=-1.0)
        v_sb = keep.tile([TOKENS, BANK], F32)
        for half in range(2):
            nc.scalar.copy(out=v_sb[:, half * (BANK // 2) : (half + 1) * (BANK // 2)], in_=v_sums[half][:, 0 : BANK // 2])
        rotate(0, [(head[:, 0:NARROW], 0, NARROW // 2), (whole[:, NARROW:BANK], NARROW // 2, (BANK - NARROW) // 2)])
        rotate(1, [(sums[1][:, 0 : BANK // 2], 0, PAIRS // 2), (sums[1][:, BANK // 2 : BANK], PAIRS // 2, PAIRS // 2)])
        nc.sync.dma_start(out=bank_out[BANKS - 1], in_=v_sb[:])
        rotate(2, [(sums[2][:], 0, PAIRS)])
